import numpy as np
import ml_dtypes


def mxq(x, axis, fmt="e4m3"):
    dtype, down = {"e4m3": (ml_dtypes.float8_e4m3fn, 7), "e5m2": (ml_dtypes.float8_e5m2, 14)}[fmt]
    v = np.moveaxis(np.asarray(x, np.float32).astype(ml_dtypes.bfloat16).astype(np.float64), axis, -1)
    blocks = v.reshape(v.shape[:-1] + (-1, 32))
    amax = np.abs(blocks).max(-1, keepdims=True)
    byte = np.maximum(np.where(amax > 0, np.frexp(amax)[1] - 1 + 127, 0) - down, 1)
    scale = np.exp2(byte - 127.0)
    codes = (blocks / scale).astype(np.float32).astype(dtype).astype(np.float64)
    return np.moveaxis((codes * scale).reshape(v.shape), -1, axis)


WIDE = False


def mx_kscale(k):
    if not WIDE:
        return np.ones(k)
    levels = np.array([10, -10, 5, -5, 0])
    if k % 512:
        return np.exp2(np.random.permutation(np.resize(levels, k // 32))).repeat(32)
    a = np.empty((k // 512, 16))
    for p in range(k // 512):
        a[p, :8] = np.random.permutation(np.resize(levels, 8))
        for g in range(8):
            far = levels[np.abs(levels - a[p, g]) >= 10]
            a[p, g + 8] = far[np.random.randint(len(far))]
    return np.exp2(a.ravel()).repeat(32)


BF16 = ml_dtypes.bfloat16


def bf(x):
    return np.asarray(x, np.float32).astype(BF16)


def f64(x):
    return np.asarray(x).astype(np.float64)


BATCH, ROWS, COLS, IN_DIM, OUT_DIM = 2, 32, 32, 512, 128
N = ROWS * COLS
EPS_BN = 1e-5
EPS_DEG = 1e-5


def _stencil9(x):
    R, C = x.shape[-3], x.shape[-2]
    pad = [(0, 0)] * (x.ndim - 3) + [(1, 1), (1, 1), (0, 0)]
    xp = np.pad(x, pad)
    out = np.zeros_like(x)
    for di in range(3):
        for dj in range(3):
            out = out + xp[..., di:di + R, dj:dj + C, :]
    return out


def _deg_inv_sqrt(rows, cols):
    D = _stencil9(np.ones((rows, cols, 1)))[..., 0]
    return (D + EPS_DEG) ** -0.5


def setup_inputs():
    s = mx_kscale(IN_DIM)
    mu = 0.5 * np.random.standard_normal(IN_DIM)
    bound = np.sqrt(6.0 / IN_DIM)
    return {"H": bf((np.random.standard_normal((BATCH, N, IN_DIM)) + mu) * s),
            "W": bf(np.random.uniform(-bound, bound, (IN_DIM, OUT_DIM)) / s[:, None]),
            "gamma": bf(1.0 + 0.1 * np.random.standard_normal(OUT_DIM)),
            "beta": bf(0.2 * np.random.standard_normal(OUT_DIM))}


def reference(H, W, gamma, beta):
    B, n_nodes, _ = H.shape
    Ht = mxq(f64(H), 2, "e4m3") @ mxq(f64(W), 0, "e4m3")
    mean = Ht.mean(axis=(0, 1))
    var = Ht.var(axis=(0, 1))
    Ht = (Ht - mean) * (1.0 / np.sqrt(var + EPS_BN)) * f64(gamma) + f64(beta)
    Ht = np.maximum(Ht, 0.0)
    d = _deg_inv_sqrt(ROWS, COLS)[None, :, :, None]
    Hg = Ht.reshape(B, ROWS, COLS, OUT_DIM)
    Hagg = d * _stencil9(Hg * d)
    return Hagg.reshape(B, n_nodes, OUT_DIM)

@@ -1,0 +1,245 @@
+import concourse.mybir as mybir
+from concourse.masks import make_identity
+
+F32 = mybir.dt.float32
+BF16 = mybir.dt.bfloat16
+U32 = mybir.dt.uint32
+U8 = mybir.dt.uint8
+FP8X4 = mybir.dt.float8_e4m3fn_x4
+ACT = mybir.ActivationFunctionType
+ALU = mybir.AluOpType
+
+P = 128
+BATCH, ROWS, COLS, IN_DIM, OUT_DIM = 2, 32, 32, 512, 128
+NODES = BATCH * ROWS * COLS
+EPS_BN = 1e-5
+EPS_DEG = 1e-5
+
+FLOPS = 2 * NODES * IN_DIM * OUT_DIM
+
+CHUNK = 512
+CHUNKS = NODES // CHUNK
+CHUNK_ROWS = CHUNK // COLS
+PER_PART = CHUNK // P
+WORDS = IN_DIM // 2
+
+D_INSIDE = (9 + EPS_DEG) ** -0.5
+D_EDGE = (6 + EPS_DEG) ** -0.5
+D_CORNER = (4 + EPS_DEG) ** -0.5
+
+HALF_COLS = COLS // 2
+GROUP_ROWS = P // HALF_COLS
+GROUPS = NODES // (2 * P)
+GROUPS_PER_IMAGE = GROUPS // BATCH
+TOP, MIDDLE, BOTTOM = 0, 1, 2
+
+
+def group_kind(g):
+    if g % GROUPS_PER_IMAGE == 0:
+        return TOP
+    if g % GROUPS_PER_IMAGE == GROUPS_PER_IMAGE - 1:
+        return BOTTOM
+    return MIDDLE
+
+
+def tile_graphconvolutionbatch_s_kernel(tc, H, W, gamma, beta, out):
+    nc = tc.nc
+    h_rows = H.flatten_outer_dims()
+    out_groups = out.flatten_outer_dims().rearrange("(g p two) f -> p g (two f)", p=P, two=2)
+
+    with (
+        tc.tile_pool(name="keep", bufs=1) as keep,
+        tc.psum_pool(name="psum", bufs=8) as psum,
+        tc.manual_schedule(),
+    ):
+        w_raw = keep.tile([P, 4, OUT_DIM], BF16)
+        nc.scalar.dma_start(
+            out=w_raw[:].rearrange("q t c -> q (t c)"),
+            in_=W.rearrange("(q t) c -> q (t c)", t=4),
+        )
+        h_sb = keep.tile([P, CHUNKS * PER_PART * IN_DIM], BF16)
+        for j in range(CHUNKS):
+            chunk_rows = h_rows[j * CHUNK : (j + 1) * CHUNK, :].rearrange("(p t) k -> p t k", t=PER_PART)
+            for h in range(2):
+                first_col = (j * PER_PART + 2 * h) * IN_DIM
+                nc.sync.dma_start(
+                    out=h_sb[:, first_col : first_col + 2 * IN_DIM],
+                    in_=chunk_rows[:, 2 * h : 2 * h + 2, :].rearrange("p t k -> p (t k)"),
+                )
+        gamma_bf = keep.tile([P, 1], BF16)
+        beta_bf = keep.tile([P, 1], BF16)
+        nc.sync.dma_start(out=gamma_bf[:], in_=gamma.rearrange("(p o) -> p o", o=1))
+        nc.sync.dma_start(out=beta_bf[:], in_=beta.rearrange("(p o) -> p o", o=1))
+
+        ident = keep.tile([P, P], F32)
+        make_identity(nc, ident[:])
+        eps_bn = keep.tile([P, 1], F32)
+        eps_deg = keep.tile([P, 1], F32)
+        nc.vector.memset(eps_bn[:], EPS_BN)
+        nc.vector.memset(eps_deg[:], EPS_DEG)
+        table_warm = keep.tile([P, 1], F32)
+        nc.scalar.activation(out=table_warm[:], in_=eps_bn[:], func=ACT.Abs_reciprocal_sqrt)
+
+        relu_d = [keep.tile([P, ROWS, COLS + 2], F32, name="relu_d%d" % b) for b in range(BATCH)]
+        col_sums = [keep.tile([P, 2, ROWS + 2, HALF_COLS], F32, name="col_sums%d" % b) for b in range(BATCH)]
+        for b in range(BATCH):
+            nc.vector.memset(relu_d[b][:, :, 0 : COLS + 2 : COLS + 1], 0.0)
+            nc.vector.memset(col_sums[b][:, :, 0 : ROWS + 2 : ROWS + 1, :], 0.0)
+
+        degree = keep.tile([P, 2, 3, GROUP_ROWS, HALF_COLS], F32)
+        nc.vector.memset(degree[:], 9.0)
+        nc.vector.memset(degree[:, 0, :, :, 0], 6.0)
+        nc.vector.memset(degree[:, 1, :, :, HALF_COLS - 1], 6.0)
+        nc.vector.memset(degree[:, :, TOP, 0, :], 6.0)
+        nc.vector.memset(degree[:, :, BOTTOM, GROUP_ROWS - 1, :], 6.0)
+        for kind, row in ((TOP, 0), (BOTTOM, GROUP_ROWS - 1)):
+            nc.vector.memset(degree[:, 0, kind, row, 0:1], 4.0)
+            nc.vector.memset(degree[:, 1, kind, row, HALF_COLS - 1 : HALF_COLS], 4.0)
+
+        w_grouped = keep.tile([P, OUT_DIM, 4], BF16, align_bytes=64)
+        w_codes = keep.tile([P, OUT_DIM], U32, align_bytes=64)
+        w_scales = keep.tile([P, OUT_DIM], U8, align_bytes=64)
+        nc.vector.tensor_copy(out=w_grouped[:], in_=w_raw[:].rearrange("q t c -> q c t"))
+        nc.vector.quantize_mx(
+            out=w_codes[:].bitcast(FP8X4), scales=w_scales[:], in_=w_grouped[:].rearrange("q c t -> q (c t)")
+        )
+
+        h_words = h_sb[:].bitcast(F32).rearrange("p (j t w u) -> p j t u w", j=CHUNKS, t=PER_PART, u=2)
+        h_grouped = keep.tile([P, NODES * 4], BF16, align_bytes=64)
+        h_grouped_words = h_grouped[:].bitcast(F32).rearrange(
+            "q (j t p u) -> q j t p u", j=CHUNKS, t=PER_PART, u=2
+        )
+        h_codes = keep.tile([P, NODES], U32, align_bytes=64)
+        h_scales = keep.tile([P, NODES], U8, align_bytes=64)
+        stats = keep.tile([P, CHUNKS, 6], F32)
+        y = []
+        half = CHUNK // 2
+
+        def turn_and_quantise(j):
+            for h in range(2):
+                h_t = psum.tile([P, 2, 2, P], F32, tag="bank")
+                for t in range(2):
+                    for u in range(2):
+                        nc.tensor.transpose(h_t[:, t, u, :], h_words[:, j, 2 * h + t, u, :], ident[:])
+                nc.scalar.copy(
+                    out=h_grouped_words[:, j, 2 * h : 2 * h + 2, :, :],
+                    in_=h_t[:].rearrange("q t u p -> q t p u"),
+                )
+                first = j * CHUNK + h * half
+                nc.vector.quantize_mx(
+                    out=h_codes[:, first : first + half].bitcast(FP8X4),
+                    scales=h_scales[:, first : first + half],
+                    in_=h_grouped[:, 4 * first : 4 * (first + half)],
+                )
+
+        def multiply(j):
+            y.append(psum.tile([P, CHUNK], F32, tag="bank", name="y%d" % j))
+            nc.tensor.matmul_mx(
+                out=y[j][:],
+                lhsT=w_codes[:].bitcast(FP8X4),
+                lhsT_scale=w_scales[:],
+                rhs=h_codes[:, j * CHUNK : (j + 1) * CHUNK].bitcast(FP8X4),
+                rhs_scale=h_scales[:, j * CHUNK : (j + 1) * CHUNK],
+                start=True,
+                stop=True,
+            )
+            nc.vector.bn_stats(out=stats[:, j, :], in_=y[j][:])
+
+        for j in range(CHUNKS):
+            turn_and_quantise(j)
+        for j in range(CHUNKS):
+            multiply(j)
+
+        gamma_d = keep.tile([P, 1], F32)
+        minus_gamma_d = keep.tile([P, 1], F32)
+        beta_d = keep.tile([P, 1], F32)
+        nc.gpsimd.tensor_scalar_mul(out=gamma_d[:], in0=gamma_bf[:], scalar1=D_INSIDE)
+        nc.gpsimd.tensor_scalar_mul(out=minus_gamma_d[:], in0=gamma_bf[:], scalar1=-D_INSIDE)
+        nc.gpsimd.tensor_scalar_mul(out=beta_d[:], in0=beta_bf[:], scalar1=D_INSIDE)
+
+        degree_t = [psum.tile([P, 3, P], F32, tag="bank", name="degree_t%d" % par) for par in range(2)]
+        for par in range(2):
+            for kind in (TOP, MIDDLE, BOTTOM):
+                nc.tensor.transpose(
+                    degree_t[par][:, kind, :], degree[:, par, kind, :, :].rearrange("f r m -> f (r m)"), ident[:]
+                )
+
+        mean_var = keep.tile([P, 2], F32)
+        nc.vector.bn_aggr(out=mean_var[:], in_=stats[:].rearrange("f j s -> f (j s)"))
+        rstd = keep.tile([P, 1], F32)
+        minus_mean_gamma_d = keep.tile([P, 1], F32)
+        scale = keep.tile([P, 1], F32)
+        bias = keep.tile([P, 1], F32)
+        nc.scalar.activation(out=rstd[:], in_=mean_var[:, 1:2], func=ACT.Abs_reciprocal_sqrt, bias=eps_bn[:])
+        nc.vector.tensor_mul(out=minus_mean_gamma_d[:], in0=mean_var[:, 0:1], in1=minus_gamma_d[:])
+        nc.vector.tensor_mul(out=scale[:], in0=gamma_d[:], in1=rstd[:])
+        nc.vector.scalar_tensor_tensor(
+            out=bias[:], in0=minus_mean_gamma_d[:], scalar=rstd[:], in1=beta_d[:], op0=ALU.mult, op1=ALU.add
+        )
+
+        last = COLS + 1
+        for j in range(CHUNKS):
+            rows = slice((j % 2) * CHUNK_ROWS, (j % 2 + 1) * CHUNK_ROWS)
+            nc.scalar.activation(
+                out=relu_d[j // 2][:, rows, 1:last].rearrange("f r (q t) -> f r q t", t=PER_PART),
+                in_=y[j][:].rearrange("f (t r q) -> f r q t", t=PER_PART, r=CHUNK_ROWS),
+                func=ACT.Relu,
+                scale=scale[:],
+                bias=bias[:],
+            )
+        d_out = keep.tile([P, 3, 2], F32)
+        for par in range(2):
+            nc.scalar.activation(
+                out=d_out[:, :, par], in_=degree_t[par][:, :, 0], func=ACT.Abs_reciprocal_sqrt, bias=eps_deg[:]
+            )
+
+        pair = keep.tile([P, CHUNKS, CHUNK_ROWS, HALF_COLS], F32)
+
+        def border(j):
+            x = relu_d[j // 2]
+            edge_row = 0 if j % 2 == 0 else ROWS - 1
+            other_rows = slice(1, CHUNK_ROWS) if j % 2 == 0 else slice(CHUNK_ROWS, ROWS - 1)
+            for region, factor in (
+                (x[:, edge_row, 2 : last - 1], D_EDGE / D_INSIDE),
+                (x[:, other_rows, 1 : last : COLS - 1], D_EDGE / D_INSIDE),
+                (x[:, edge_row, 1 : last : COLS - 1], D_CORNER / D_INSIDE),
+            ):
+                nc.vector.tensor_scalar_mul(out=region, in0=region, scalar1=factor)
+
+        border(0)
+        for j in range(CHUNKS):
+            x = relu_d[j // 2]
+            rows = slice((j % 2) * CHUNK_ROWS, (j % 2 + 1) * CHUNK_ROWS)
+            padded_rows = slice(1 + (j % 2) * CHUNK_ROWS, 1 + (j % 2 + 1) * CHUNK_ROWS)
+            nc.vector.tensor_add(out=pair[:, j, :, :], in0=x[:, rows, 1:last:2], in1=x[:, rows, 2 : last + 1 : 2])
+            nc.vector.tensor_add(
+                out=col_sums[j // 2][:, 0, padded_rows, :], in0=pair[:, j, :, :], in1=x[:, rows, 0 : last - 1 : 2]
+            )
+            if j + 1 < CHUNKS:
+                border(j + 1)
+            nc.vector.tensor_add(
+                out=col_sums[j // 2][:, 1, padded_rows, :], in0=pair[:, j, :, :], in1=x[:, rows, 3 : last + 1 : 2]
+            )
+
+        out_sb = keep.tile([P, GROUPS, 2, OUT_DIM], F32)
+        for g in range(GROUPS):
+            top = (g % GROUPS_PER_IMAGE) * GROUP_ROWS
+            for par in range(2):
+                box_t = psum.tile([P, OUT_DIM], F32, tag="bank")
+                for dr in range(3):
+                    nc.tensor.matmul(
+                        out=box_t[:],
+                        lhsT=col_sums[g // GROUPS_PER_IMAGE][:, par, top + dr : top + dr + GROUP_ROWS, :].rearrange(
+                            "f r m -> f (r m)"
+                        ),
+                        rhs=ident[:],
+                        is_transpose=True,
+                        start=(dr == 0),
+                        stop=(dr == 2),
+                    )
+                d_col = d_out[:, group_kind(g), par : par + 1]
+                if par == 0:
+                    nc.scalar.activation(out=out_sb[:, g, par, :], in_=box_t[:], func=ACT.Copy, scale=d_col)
+                else:
+                    nc.vector.tensor_scalar_mul(out=out_sb[:, g, par, :], in0=box_t[:], scalar1=d_col)
+            nc.sync.dma_start(out=out_groups[:, g, :], in_=out_sb[:, g, :, :].rearrange("p two f -> p (two f)"))

@@ -17,20 +17,25 @@ EPS_DEG = 1e-5
 
 FLOPS = 2 * NODES * IN_DIM * OUT_DIM
 
-CHUNK = 512
+HALF_COLS = COLS // 2
+GROUP = 2 * P
+GROUPS = NODES // GROUP
+GROUP_ROWS = GROUP // COLS
+GROUPS_PER_IMAGE = GROUPS // BATCH
+CHUNK = 2 * GROUP
 CHUNKS = NODES // CHUNK
 CHUNK_ROWS = CHUNK // COLS
-PER_PART = CHUNK // P
 WORDS = IN_DIM // 2
 
-D_INSIDE = (9 + EPS_DEG) ** -0.5
-D_EDGE = (6 + EPS_DEG) ** -0.5
-D_CORNER = (4 + EPS_DEG) ** -0.5
+D_KINDS = ((9 + EPS_DEG) ** -0.5, (6 + EPS_DEG) ** -0.5, (4 + EPS_DEG) ** -0.5)
+INSIDE, EDGE, CORNER = 0, 1, 2
 
-HALF_COLS = COLS // 2
-GROUP_ROWS = P // HALF_COLS
-GROUPS = NODES // (2 * P)
-GROUPS_PER_IMAGE = GROUPS // BATCH
+EVEN = 4
+ODD = 24
+X_WIDTH = 44
+
+VECTOR_COPIES = (1,)
+
 TOP, MIDDLE, BOTTOM = 0, 1, 2
 
 
@@ -49,27 +54,29 @@ def tile_graphconvolutionbatch_s_kernel(tc, H, W, gamma, beta, out):
 
     with (
         tc.tile_pool(name="keep", bufs=1) as keep,
-        tc.psum_pool(name="psum", bufs=8) as psum,
+        tc.psum_pool(name="psum", bufs=4) as psum,
         tc.manual_schedule(),
     ):
         w_raw = keep.tile([P, 4, OUT_DIM], BF16)
         nc.scalar.dma_start(
-            out=w_raw[:].rearrange("q t c -> q (t c)"),
-            in_=W.rearrange("(q t) c -> q (t c)", t=4),
+            out=w_raw[:].rearrange("q t c -> q (t c)"), in_=W.rearrange("(q t) c -> q (t c)", t=4)
         )
-        h_sb = keep.tile([P, CHUNKS * PER_PART * IN_DIM], BF16)
-        for j in range(CHUNKS):
-            chunk_rows = h_rows[j * CHUNK : (j + 1) * CHUNK, :].rearrange("(p t) k -> p t k", t=PER_PART)
-            for h in range(2):
-                first_col = (j * PER_PART + 2 * h) * IN_DIM
-                nc.sync.dma_start(
-                    out=h_sb[:, first_col : first_col + 2 * IN_DIM],
-                    in_=chunk_rows[:, 2 * h : 2 * h + 2, :].rearrange("p t k -> p (t k)"),
-                )
+        h_sb = keep.tile([P, GROUPS, 2 * IN_DIM], BF16)
+        for g in range(GROUPS):
+            nc.sync.dma_start(
+                out=h_sb[:, g, :],
+                in_=h_rows[g * GROUP : (g + 1) * GROUP, :].rearrange("(p t) k -> p (t k)", t=2),
+            )
         gamma_bf = keep.tile([P, 1], BF16)
         beta_bf = keep.tile([P, 1], BF16)
         nc.sync.dma_start(out=gamma_bf[:], in_=gamma.rearrange("(p o) -> p o", o=1))
         nc.sync.dma_start(out=beta_bf[:], in_=beta.rearrange("(p o) -> p o", o=1))
+
+        zeros = keep.tile([P, P], F32)
+        nc.vector.memset(zeros[:], 0.0)
+        idle_work = psum.tile([P, 4, P], F32, tag="product", name="idle_work")
+        for i in range(4):
+            nc.tensor.matmul(out=idle_work[:, i, :], lhsT=zeros[:], rhs=zeros[:], start=True, stop=True)
 
         ident = keep.tile([P, P], F32)
         make_identity(nc, ident[:])
@@ -80,21 +87,31 @@ def tile_graphconvolutionbatch_s_kernel(tc, H, W, gamma, beta, out):
         table_warm = keep.tile([P, 1], F32)
         nc.scalar.activation(out=table_warm[:], in_=eps_bn[:], func=ACT.Abs_reciprocal_sqrt)
 
-        relu_d = [keep.tile([P, ROWS, COLS + 2], F32, name="relu_d%d" % b) for b in range(BATCH)]
+        border = keep.tile([P, 5], F32)
+        nc.vector.memset(border[:], 0.0)
+        first_row, last_row = slice(0, HALF_COLS), slice(P - HALF_COLS, P)
+        for column, members in enumerate(
+            (slice(0, P, HALF_COLS), slice(HALF_COLS - 1, P, HALF_COLS), first_row, None, last_row)
+        ):
+            if members is not None:
+                nc.vector.reduce_sum(
+                    out=border[:, column : column + 1], in_=ident[:, members], axis=mybir.AxisListType.X
+                )
+        nc.vector.tensor_scalar(out=border[:], in0=border[:], scalar1=-1.0, scalar2=3.0, op0=ALU.mult, op1=ALU.add)
+        degree = keep.tile([P, 3, 2], F32)
+        nc.vector.tensor_mul(
+            out=degree[:],
+            in0=border[:, 2:5].unsqueeze(2).to_broadcast([P, 3, 2]),
+            in1=border[:, 0:2].unsqueeze(1).to_broadcast([P, 3, 2]),
+        )
+        d_out = keep.tile([P, 3, 2], F32)
+        nc.scalar.activation(out=d_out[:], in_=degree[:], func=ACT.Abs_reciprocal_sqrt, bias=eps_deg[:])
+
+        x = [keep.tile([P, ROWS, X_WIDTH], F32, name="x%d" % b) for b in range(BATCH)]
         col_sums = [keep.tile([P, 2, ROWS + 2, HALF_COLS], F32, name="col_sums%d" % b) for b in range(BATCH)]
         for b in range(BATCH):
-            nc.vector.memset(relu_d[b][:, :, 0 : COLS + 2 : COLS + 1], 0.0)
-            nc.vector.memset(col_sums[b][:, :, 0 : ROWS + 2 : ROWS + 1, :], 0.0)
-
-        degree = keep.tile([P, 2, 3, GROUP_ROWS, HALF_COLS], F32)
-        nc.vector.memset(degree[:], 9.0)
-        nc.vector.memset(degree[:, 0, :, :, 0], 6.0)
-        nc.vector.memset(degree[:, 1, :, :, HALF_COLS - 1], 6.0)
-        nc.vector.memset(degree[:, :, TOP, 0, :], 6.0)
-        nc.vector.memset(degree[:, :, BOTTOM, GROUP_ROWS - 1, :], 6.0)
-        for kind, row in ((TOP, 0), (BOTTOM, GROUP_ROWS - 1)):
-            nc.vector.memset(degree[:, 0, kind, row, 0:1], 4.0)
-            nc.vector.memset(degree[:, 1, kind, row, HALF_COLS - 1 : HALF_COLS], 4.0)
+            nc.gpsimd.memset(x[b][:, :, EVEN + HALF_COLS : ODD], 0.0)
+            nc.gpsimd.memset(col_sums[b][:, :, 0 : ROWS + 2 : ROWS + 1, :], 0.0)
 
         w_grouped = keep.tile([P, OUT_DIM, 4], BF16, align_bytes=64)
         w_codes = keep.tile([P, OUT_DIM], U32, align_bytes=64)
@@ -104,38 +121,36 @@ def tile_graphconvolutionbatch_s_kernel(tc, H, W, gamma, beta, out):
             out=w_codes[:].bitcast(FP8X4), scales=w_scales[:], in_=w_grouped[:].rearrange("q c t -> q (c t)")
         )
 
-        h_words = h_sb[:].bitcast(F32).rearrange("p (j t w u) -> p j t u w", j=CHUNKS, t=PER_PART, u=2)
+        h_words = h_sb[:].bitcast(F32).rearrange("p g (t w u) -> p g t u w", t=2, u=2)
         h_grouped = keep.tile([P, NODES * 4], BF16, align_bytes=64)
-        h_grouped_words = h_grouped[:].bitcast(F32).rearrange(
-            "q (j t p u) -> q j t p u", j=CHUNKS, t=PER_PART, u=2
-        )
+        h_grouped_words = h_grouped[:].bitcast(F32).rearrange("q (n u) -> q n u", u=2)
         h_codes = keep.tile([P, NODES], U32, align_bytes=64)
         h_scales = keep.tile([P, NODES], U8, align_bytes=64)
         stats = keep.tile([P, CHUNKS, 6], F32)
         y = []
-        half = CHUNK // 2
 
-        def turn_and_quantise(j):
-            for h in range(2):
-                h_t = psum.tile([P, 2, 2, P], F32, tag="bank")
-                for t in range(2):
-                    for u in range(2):
-                        nc.tensor.transpose(h_t[:, t, u, :], h_words[:, j, 2 * h + t, u, :], ident[:])
-                nc.scalar.copy(
-                    out=h_grouped_words[:, j, 2 * h : 2 * h + 2, :, :],
-                    in_=h_t[:].rearrange("q t u p -> q t p u"),
-                )
-                first = j * CHUNK + h * half
-                nc.vector.quantize_mx(
-                    out=h_codes[:, first : first + half].bitcast(FP8X4),
-                    scales=h_scales[:, first : first + half],
-                    in_=h_grouped[:, 4 * first : 4 * (first + half)],
-                )
+        def turn(g):
+            h_t = psum.tile([P, 2, GROUP_ROWS, 2, HALF_COLS], F32, tag="turn")
+            for t in range(2):
+                for u in range(2):
+                    nc.tensor.transpose(h_t[:, u, :, t, :], h_words[:, g, t, u, :], ident[:])
+            copy = nc.vector.tensor_copy if g in VECTOR_COPIES else nc.scalar.copy
+            copy(
+                out=h_grouped_words[:, g * GROUP : (g + 1) * GROUP, :],
+                in_=h_t[:].rearrange("q u r t m -> q (r t m) u"),
+            )
+
+        def quantise(g):
+            nc.vector.quantize_mx(
+                out=h_codes[:, g * GROUP : (g + 1) * GROUP].bitcast(FP8X4),
+                scales=h_scales[:, g * GROUP : (g + 1) * GROUP],
+                in_=h_grouped[:, 4 * g * GROUP : 4 * (g + 1) * GROUP],
+            )
 
         def multiply(j):
-            y.append(psum.tile([P, CHUNK], F32, tag="bank", name="y%d" % j))
+            y.append(psum.tile([P, CHUNK_ROWS, COLS], F32, tag="product", name="y%d" % j))
             nc.tensor.matmul_mx(
-                out=y[j][:],
+                out=y[j][:].rearrange("f r c -> f (r c)"),
                 lhsT=w_codes[:].bitcast(FP8X4),
                 lhsT_scale=w_scales[:],
                 rhs=h_codes[:, j * CHUNK : (j + 1) * CHUNK].bitcast(FP8X4),
@@ -143,103 +158,149 @@ def tile_graphconvolutionbatch_s_kernel(tc, H, W, gamma, beta, out):
                 start=True,
                 stop=True,
             )
-            nc.vector.bn_stats(out=stats[:, j, :], in_=y[j][:])
 
-        for j in range(CHUNKS):
-            turn_and_quantise(j)
-        for j in range(CHUNKS):
+        def take_statistics(j):
+            nc.vector.bn_stats(out=stats[:, j, :], in_=y[j][:].rearrange("f r c -> f (r c)"))
+
+        for g in range(GROUPS):
+            turn(g)
+            if g > 0:
+                quantise(g - 1)
+            if g in (4, 6):
+                multiply(g // 2 - 2)
+                take_statistics(g // 2 - 2)
+        quantise(GROUPS - 1)
+        for j in (2, 3):
             multiply(j)
+            take_statistics(j)
+        spare = psum.tile([P, CHUNK], F32, tag="turn", name="spare")
+        for i in range(10):
+            nc.tensor.matmul_mx(
+                out=spare[:],
+                lhsT=w_codes[:].bitcast(FP8X4),
+                lhsT_scale=w_scales[:],
+                rhs=h_codes[:, NODES - CHUNK :].bitcast(FP8X4),
+                rhs_scale=h_scales[:, NODES - CHUNK :],
+                start=True,
+                stop=True,
+            )
 
-        gamma_d = keep.tile([P, 1], F32)
-        minus_gamma_d = keep.tile([P, 1], F32)
-        beta_d = keep.tile([P, 1], F32)
-        nc.gpsimd.tensor_scalar_mul(out=gamma_d[:], in0=gamma_bf[:], scalar1=D_INSIDE)
-        nc.gpsimd.tensor_scalar_mul(out=minus_gamma_d[:], in0=gamma_bf[:], scalar1=-D_INSIDE)
-        nc.gpsimd.tensor_scalar_mul(out=beta_d[:], in0=beta_bf[:], scalar1=D_INSIDE)
-
-        degree_t = [psum.tile([P, 3, P], F32, tag="bank", name="degree_t%d" % par) for par in range(2)]
-        for par in range(2):
-            for kind in (TOP, MIDDLE, BOTTOM):
-                nc.tensor.transpose(
-                    degree_t[par][:, kind, :], degree[:, par, kind, :, :].rearrange("f r m -> f (r m)"), ident[:]
-                )
+        gamma_d = keep.tile([P, 3], F32)
+        minus_gamma_d = keep.tile([P, 3], F32)
+        beta_d = keep.tile([P, 3], F32)
+        for kind in (INSIDE, EDGE, CORNER):
+            one = slice(kind, kind + 1)
+            nc.gpsimd.tensor_scalar_mul(out=gamma_d[:, one], in0=gamma_bf[:], scalar1=D_KINDS[kind])
+            nc.gpsimd.tensor_scalar_mul(out=minus_gamma_d[:, one], in0=gamma_bf[:], scalar1=-D_KINDS[kind])
+            nc.gpsimd.tensor_scalar_mul(out=beta_d[:, one], in0=beta_bf[:], scalar1=D_KINDS[kind])
 
         mean_var = keep.tile([P, 2], F32)
         nc.vector.bn_aggr(out=mean_var[:], in_=stats[:].rearrange("f j s -> f (j s)"))
         rstd = keep.tile([P, 1], F32)
-        minus_mean_gamma_d = keep.tile([P, 1], F32)
-        scale = keep.tile([P, 1], F32)
-        bias = keep.tile([P, 1], F32)
+        minus_mean_gamma_d = keep.tile([P, 3], F32)
+        scale = keep.tile([P, 3], F32)
+        bias = keep.tile([P, 3], F32)
         nc.scalar.activation(out=rstd[:], in_=mean_var[:, 1:2], func=ACT.Abs_reciprocal_sqrt, bias=eps_bn[:])
-        nc.vector.tensor_mul(out=minus_mean_gamma_d[:], in0=mean_var[:, 0:1], in1=minus_gamma_d[:])
-        nc.vector.tensor_mul(out=scale[:], in0=gamma_d[:], in1=rstd[:])
+        nc.vector.tensor_scalar_mul(out=minus_mean_gamma_d[:], in0=minus_gamma_d[:], scalar1=mean_var[:, 0:1])
+        nc.vector.tensor_scalar_mul(out=scale[:], in0=gamma_d[:], scalar1=rstd[:])
         nc.vector.scalar_tensor_tensor(
             out=bias[:], in0=minus_mean_gamma_d[:], scalar=rstd[:], in1=beta_d[:], op0=ALU.mult, op1=ALU.add
         )
 
-        last = COLS + 1
-        for j in range(CHUNKS):
-            rows = slice((j % 2) * CHUNK_ROWS, (j % 2 + 1) * CHUNK_ROWS)
+        def relu_inner(b, rows, kind):
+            run = HALF_COLS - 1
+            step = ODD - EVEN - 1
+            chunk, first = divmod(b * ROWS + rows.start, CHUNK_ROWS)
+            y_rows = y[chunk][:, first : first + rows.stop - rows.start, :]
             nc.scalar.activation(
-                out=relu_d[j // 2][:, rows, 1:last].rearrange("f r (q t) -> f r q t", t=PER_PART),
-                in_=y[j][:].rearrange("f (t r q) -> f r q t", t=PER_PART, r=CHUNK_ROWS),
+                out=x[b][:, rows, EVEN + 1 : EVEN + 1 + 2 * step].rearrange("f r (t s) -> f r t s", t=2)[:, :, :, 0:run],
+                in_=y_rows[:, :, 1 : 1 + 2 * run].rearrange("f r (t m) -> f r t m", t=2),
                 func=ACT.Relu,
-                scale=scale[:],
-                bias=bias[:],
+                scale=scale[:, kind : kind + 1],
+                bias=bias[:, kind : kind + 1],
             )
-        d_out = keep.tile([P, 3, 2], F32)
-        for par in range(2):
+
+        def relu_outer(b, rows, kind):
+            chunk, first = divmod(b * ROWS + rows.start, CHUNK_ROWS)
+            y_rows = y[chunk][:, first : first + rows.stop - rows.start, :]
+            last = ODD + HALF_COLS - 1
             nc.scalar.activation(
-                out=d_out[:, :, par], in_=degree_t[par][:, :, 0], func=ACT.Abs_reciprocal_sqrt, bias=eps_deg[:]
+                out=x[b][:, rows, EVEN : last + 1 : last - EVEN],
+                in_=y_rows[:, :, 0 : COLS : COLS - 1],
+                func=ACT.Relu,
+                scale=scale[:, kind : kind + 1],
+                bias=bias[:, kind : kind + 1],
             )
 
-        pair = keep.tile([P, CHUNKS, CHUNK_ROWS, HALF_COLS], F32)
+        def relu(b, first, end):
+            inner = slice(max(first, 1), min(end, ROWS - 1))
+            relu_inner(b, inner, INSIDE)
+            relu_outer(b, inner, EDGE)
+            for row in (0, ROWS - 1):
+                if first <= row < end:
+                    relu_inner(b, slice(row, row + 1), EDGE)
+                    relu_outer(b, slice(row, row + 1), CORNER)
 
-        def border(j):
-            x = relu_d[j // 2]
-            edge_row = 0 if j % 2 == 0 else ROWS - 1
-            other_rows = slice(1, CHUNK_ROWS) if j % 2 == 0 else slice(CHUNK_ROWS, ROWS - 1)
-            for region, factor in (
-                (x[:, edge_row, 2 : last - 1], D_EDGE / D_INSIDE),
-                (x[:, other_rows, 1 : last : COLS - 1], D_EDGE / D_INSIDE),
-                (x[:, edge_row, 1 : last : COLS - 1], D_CORNER / D_INSIDE),
-            ):
-                nc.vector.tensor_scalar_mul(out=region, in0=region, scalar1=factor)
+        pair = keep.tile([P, BATCH, ROWS, HALF_COLS], F32)
 
-        border(0)
-        for j in range(CHUNKS):
-            x = relu_d[j // 2]
-            rows = slice((j % 2) * CHUNK_ROWS, (j % 2 + 1) * CHUNK_ROWS)
-            padded_rows = slice(1 + (j % 2) * CHUNK_ROWS, 1 + (j % 2 + 1) * CHUNK_ROWS)
-            nc.vector.tensor_add(out=pair[:, j, :, :], in0=x[:, rows, 1:last:2], in1=x[:, rows, 2 : last + 1 : 2])
+        def sum_pairs(b, first, end):
+            rows = slice(first, end)
             nc.vector.tensor_add(
-                out=col_sums[j // 2][:, 0, padded_rows, :], in0=pair[:, j, :, :], in1=x[:, rows, 0 : last - 1 : 2]
+                out=pair[:, b, rows, :], in0=x[b][:, rows, ODD : ODD + HALF_COLS], in1=x[b][:, rows, EVEN : EVEN + HALF_COLS]
             )
-            if j + 1 < CHUNKS:
-                border(j + 1)
+
+        def sum_columns(b, first, end):
+            rows = slice(first, end)
+            step = ODD - EVEN - 2
+            third = x[b][:, rows, EVEN + 1 : EVEN + 1 + 2 * step].rearrange("f r (a s) -> f a r s", a=2)
             nc.vector.tensor_add(
-                out=col_sums[j // 2][:, 1, padded_rows, :], in0=pair[:, j, :, :], in1=x[:, rows, 3 : last + 1 : 2]
+                out=col_sums[b][:, :, 1 + first : 1 + end, :],
+                in0=pair[:, b, rows, :].unsqueeze(1).to_broadcast([P, 2, end - first, HALF_COLS]),
+                in1=third[:, :, :, 0:HALF_COLS],
             )
 
         out_sb = keep.tile([P, GROUPS, 2, OUT_DIM], F32)
-        for g in range(GROUPS):
+        boxes = []
+
+        def sum_rows(g):
+            b = g // GROUPS_PER_IMAGE
             top = (g % GROUPS_PER_IMAGE) * GROUP_ROWS
+            boxes.append(psum.tile([P, 2, OUT_DIM], F32, tag="turn", name="box%d" % g))
             for par in range(2):
-                box_t = psum.tile([P, OUT_DIM], F32, tag="bank")
                 for dr in range(3):
                     nc.tensor.matmul(
-                        out=box_t[:],
-                        lhsT=col_sums[g // GROUPS_PER_IMAGE][:, par, top + dr : top + dr + GROUP_ROWS, :].rearrange(
-                            "f r m -> f (r m)"
-                        ),
+                        out=boxes[g][:, par, :],
+                        lhsT=col_sums[b][:, 1 - par, top + dr : top + dr + GROUP_ROWS, :].rearrange("f r m -> f (r m)"),
                         rhs=ident[:],
                         is_transpose=True,
                         start=(dr == 0),
                         stop=(dr == 2),
                     )
+
+        def store(g):
+            for par in range(2):
                 d_col = d_out[:, group_kind(g), par : par + 1]
-                if par == 0:
-                    nc.scalar.activation(out=out_sb[:, g, par, :], in_=box_t[:], func=ACT.Copy, scale=d_col)
+                if g % 2 == 0:
+                    nc.scalar.activation(out=out_sb[:, g, par, :], in_=boxes[g][:, par, :], func=ACT.Copy, scale=d_col)
                 else:
-                    nc.vector.tensor_scalar_mul(out=out_sb[:, g, par, :], in0=box_t[:], scalar1=d_col)
+                    nc.vector.tensor_scalar_mul(out=out_sb[:, g, par, :], in0=boxes[g][:, par, :], scalar1=d_col)
             nc.sync.dma_start(out=out_groups[:, g, :], in_=out_sb[:, g, :, :].rearrange("p two f -> p (two f)"))
+
+        relu_units = [(b, first, end) for b in range(BATCH) for first, end in ((0, 9), (9, 16), (16, 25), (25, 32))]
+        sum_units = [(b, first, end) for b in range(BATCH) for first, end in ((0, 9), (9, 17), (17, 25), (25, 32))]
+        AHEAD = 3
+        BEHIND = 2
+        for i in range(AHEAD):
+            relu(*relu_units[i])
+        sum_pairs(*sum_units[0])
+        for g in range(GROUPS):
+            if g + AHEAD < GROUPS:
+                relu(*relu_units[g + AHEAD])
+            if g + 1 < GROUPS:
+                sum_pairs(*sum_units[g + 1])
+            sum_columns(*sum_units[g])
+            sum_rows(g)
+            if g >= BEHIND:
+                store(g - BEHIND)
+        for g in range(GROUPS - BEHIND, GROUPS):
+            store(g)

@@ -75,7 +75,7 @@ def tile_graphconvolutionbatch_s_kernel(tc, H, W, gamma, beta, out):
         zeros = keep.tile([P, P], F32)
         nc.vector.memset(zeros[:], 0.0)
         idle_work = psum.tile([P, 4, P], F32, tag="product", name="idle_work")
-        for i in range(4):
+        for i in range(3):
             nc.tensor.matmul(out=idle_work[:, i, :], lhsT=zeros[:], rhs=zeros[:], start=True, stop=True)
 
         ident = keep.tile([P, P], F32)
@@ -174,7 +174,7 @@ def tile_graphconvolutionbatch_s_kernel(tc, H, W, gamma, beta, out):
             multiply(j)
             take_statistics(j)
         spare = psum.tile([P, CHUNK], F32, tag="turn", name="spare")
-        for i in range(10):
+        for i in range(13):
             nc.tensor.matmul_mx(
                 out=spare[:],
                 lhsT=w_codes[:].bitcast(FP8X4),
@@ -233,9 +233,9 @@ def tile_graphconvolutionbatch_s_kernel(tc, H, W, gamma, beta, out):
             )
 
         def relu(b, first, end):
-            inner = slice(max(first, 1), min(end, ROWS - 1))
-            relu_inner(b, inner, INSIDE)
-            relu_outer(b, inner, EDGE)
+            relu_inner(b, slice(max(first, 1), min(end, ROWS - 1)), INSIDE)
+            if first % CHUNK_ROWS == 0:
+                relu_outer(b, slice(max(first, 1), min(first + CHUNK_ROWS, ROWS - 1)), EDGE)
             for row in (0, ROWS - 1):
                 if first <= row < end:
                     relu_inner(b, slice(row, row + 1), EDGE)
@@ -265,11 +265,17 @@ def tile_graphconvolutionbatch_s_kernel(tc, H, W, gamma, beta, out):
         def sum_rows(g):
             b = g // GROUPS_PER_IMAGE
             top = (g % GROUPS_PER_IMAGE) * GROUP_ROWS
-            boxes.append(psum.tile([P, 2, OUT_DIM], F32, tag="turn", name="box%d" % g))
+            if g < GROUPS - 1:
+                both = psum.tile([P, 2, OUT_DIM], F32, tag="turn", name="box%d" % g)
+                boxes.append([both[:, par, :] for par in range(2)])
+            else:
+                even = psum.tile([P, OUT_DIM], F32, tag="turn", name="box_even")
+                odd = psum.tile([P, OUT_DIM], F32, tag="product", name="box_odd")
+                boxes.append([even[:], odd[:]])
             for par in range(2):
                 for dr in range(3):
                     nc.tensor.matmul(
-                        out=boxes[g][:, par, :],
+                        out=boxes[g][par],
                         lhsT=col_sums[b][:, 1 - par, top + dr : top + dr + GROUP_ROWS, :].rearrange("f r m -> f (r m)"),
                         rhs=ident[:],
                         is_transpose=True,
@@ -279,27 +285,37 @@ def tile_graphconvolutionbatch_s_kernel(tc, H, W, gamma, beta, out):
 
         def store(g):
             for par in range(2):
+                on_scalar = g % 2 == 0 if g < GROUPS - 1 else par == 0
                 d_col = d_out[:, group_kind(g), par : par + 1]
-                if g % 2 == 0:
-                    nc.scalar.activation(out=out_sb[:, g, par, :], in_=boxes[g][:, par, :], func=ACT.Copy, scale=d_col)
+                if on_scalar:
+                    nc.scalar.activation(out=out_sb[:, g, par, :], in_=boxes[g][par], func=ACT.Copy, scale=d_col)
                 else:
-                    nc.vector.tensor_scalar_mul(out=out_sb[:, g, par, :], in0=boxes[g][:, par, :], scalar1=d_col)
+                    nc.vector.tensor_scalar_mul(out=out_sb[:, g, par, :], in0=boxes[g][par], scalar1=d_col)
             nc.sync.dma_start(out=out_groups[:, g, :], in_=out_sb[:, g, :, :].rearrange("p two f -> p (two f)"))
 
-        relu_units = [(b, first, end) for b in range(BATCH) for first, end in ((0, 9), (9, 16), (16, 25), (25, 32))]
-        sum_units = [(b, first, end) for b in range(BATCH) for first, end in ((0, 9), (9, 17), (17, 25), (25, 32))]
-        AHEAD = 3
+        relu_rows = ((0, 9), (9, 16), (16, 25), (25, 32))
+        sum_rows_of_group = ((0, 9), (9, 17), (17, 25), (25, 32))
+        relu_units = [(b, first, end) for b in range(BATCH) for first, end in relu_rows]
+        sum_units = [(b, first, end) for b in range(BATCH) for first, end in sum_rows_of_group]
+        relu_units = [(0, 0, 5), (0, 5, 9)] + relu_units[1:]
+        sum_units = [(0, 0, 5), (0, 5, 9)] + sum_units[1:]
+        AHEAD = 4
         BEHIND = 2
-        for i in range(AHEAD):
-            relu(*relu_units[i])
+        for unit in relu_units[:AHEAD]:
+            relu(*unit)
         sum_pairs(*sum_units[0])
-        for g in range(GROUPS):
-            if g + AHEAD < GROUPS:
-                relu(*relu_units[g + AHEAD])
-            if g + 1 < GROUPS:
-                sum_pairs(*sum_units[g + 1])
-            sum_columns(*sum_units[g])
-            sum_rows(g)
+        sum_pairs(*sum_units[1])
+        for i in range(len(sum_units)):
+            if i + AHEAD < len(relu_units):
+                relu(*relu_units[i + AHEAD])
+            if 1 < i < len(sum_units) - 1:
+                sum_pairs(*sum_units[i + 1])
+            sum_columns(*sum_units[i])
+            if i == 1:
+                sum_pairs(*sum_units[2])
+            g = i - 1
+            if g >= 0:
+                sum_rows(g)
             if g >= BEHIND:
                 store(g - BEHIND)
         for g in range(GROUPS - BEHIND, GROUPS):

@@ -232,10 +232,14 @@ def tile_graphconvolutionbatch_s_kernel(tc, H, W, gamma, beta, out):
                 bias=bias[:, kind : kind + 1],
             )
 
+        outer_done = []
+
         def relu(b, first, end):
             relu_inner(b, slice(max(first, 1), min(end, ROWS - 1)), INSIDE)
-            if first % CHUNK_ROWS == 0:
-                relu_outer(b, slice(max(first, 1), min(first + CHUNK_ROWS, ROWS - 1)), EDGE)
+            bank = (first // CHUNK_ROWS) * CHUNK_ROWS
+            if (b, bank) not in outer_done:
+                outer_done.append((b, bank))
+                relu_outer(b, slice(max(bank, 1), min(bank + CHUNK_ROWS, ROWS - 1)), EDGE)
             for row in (0, ROWS - 1):
                 if first <= row < end:
                     relu_inner(b, slice(row, row + 1), EDGE)
@@ -266,12 +270,12 @@ def tile_graphconvolutionbatch_s_kernel(tc, H, W, gamma, beta, out):
             b = g // GROUPS_PER_IMAGE
             top = (g % GROUPS_PER_IMAGE) * GROUP_ROWS
             if g < GROUPS - 1:
-                both = psum.tile([P, 2, OUT_DIM], F32, tag="turn", name="box%d" % g)
-                boxes.append([both[:, par, :] for par in range(2)])
+                both = psum.tile([P, 2, OUT_DIM], F32, tag="turn", name="box%d" % g)[:]
+                boxes.append((both[:, 0, :], both[:, 1, :], both))
             else:
                 even = psum.tile([P, OUT_DIM], F32, tag="turn", name="box_even")
                 odd = psum.tile([P, OUT_DIM], F32, tag="product", name="box_odd")
-                boxes.append([even[:], odd[:]])
+                boxes.append((even[:], odd[:], None))
             for par in range(2):
                 for dr in range(3):
                     nc.tensor.matmul(
@@ -284,13 +288,22 @@ def tile_graphconvolutionbatch_s_kernel(tc, H, W, gamma, beta, out):
                     )
 
         def store(g):
-            for par in range(2):
-                on_scalar = g % 2 == 0 if g < GROUPS - 1 else par == 0
-                d_col = d_out[:, group_kind(g), par : par + 1]
-                if on_scalar:
-                    nc.scalar.activation(out=out_sb[:, g, par, :], in_=boxes[g][par], func=ACT.Copy, scale=d_col)
-                else:
-                    nc.vector.tensor_scalar_mul(out=out_sb[:, g, par, :], in0=boxes[g][par], scalar1=d_col)
+            even, odd, both = boxes[g]
+            d = d_out[:, group_kind(g), :]
+
+            def scaled_on_scalar(par, box):
+                nc.scalar.activation(out=out_sb[:, g, par, :], in_=box, func=ACT.Copy, scale=d[:, par : par + 1])
+
+            if g == GROUPS - 1:
+                scaled_on_scalar(0, even)
+                nc.vector.tensor_scalar_mul(out=out_sb[:, g, 1, :], in0=odd, scalar1=d[:, 1:2])
+            elif g in (1, 4):
+                scaled_on_scalar(0, even)
+                scaled_on_scalar(1, odd)
+            else:
+                nc.vector.tensor_mul(
+                    out=out_sb[:, g, :, :], in0=both, in1=d.unsqueeze(2).to_broadcast([P, 2, OUT_DIM])
+                )
             nc.sync.dma_start(out=out_groups[:, g, :], in_=out_sb[:, g, :, :].rearrange("p two f -> p (two f)"))
 
         relu_rows = ((0, 9), (9, 16), (16, 25), (25, 32))

@@ -174,7 +174,7 @@ def tile_graphconvolutionbatch_s_kernel(tc, H, W, gamma, beta, out):
             multiply(j)
             take_statistics(j)
         spare = psum.tile([P, CHUNK], F32, tag="turn", name="spare")
-        for i in range(13):
+        for i in range(9):
             nc.tensor.matmul_mx(
                 out=spare[:],
                 lhsT=w_codes[:].bitcast(FP8X4),
@@ -184,6 +184,9 @@ def tile_graphconvolutionbatch_s_kernel(tc, H, W, gamma, beta, out):
                 start=True,
                 stop=True,
             )
+
+        def keep_busy(values):
+            nc.tensor.matmul(out=spare[:, 0:P], lhsT=zeros[:], rhs=values, start=True, stop=True)
 
         gamma_d = keep.tile([P, 3], F32)
         minus_gamma_d = keep.tile([P, 3], F32)
@@ -316,8 +319,10 @@ def tile_graphconvolutionbatch_s_kernel(tc, H, W, gamma, beta, out):
         BEHIND = 2
         for unit in relu_units[:AHEAD]:
             relu(*unit)
+        keep_busy(x[0][:, 1:5, EVEN : EVEN + COLS])
         sum_pairs(*sum_units[0])
         sum_pairs(*sum_units[1])
+        keep_busy(pair[:, 0, 0:8, :])
         for i in range(len(sum_units)):
             if i + AHEAD < len(relu_units):
                 relu(*relu_units[i + AHEAD])

@@ -74,10 +74,6 @@ def tile_graphconvolutionbatch_s_kernel(tc, H, W, gamma, beta, out):
 
         zeros = keep.tile([P, P], F32)
         nc.vector.memset(zeros[:], 0.0)
-        idle_work = psum.tile([P, 4, P], F32, tag="product", name="idle_work")
-        for i in range(3):
-            nc.tensor.matmul(out=idle_work[:, i, :], lhsT=zeros[:], rhs=zeros[:], start=True, stop=True)
-
         ident = keep.tile([P, P], F32)
         make_identity(nc, ident[:])
         eps_bn = keep.tile([P, 1], F32)
@@ -174,7 +170,7 @@ def tile_graphconvolutionbatch_s_kernel(tc, H, W, gamma, beta, out):
             multiply(j)
             take_statistics(j)
         spare = psum.tile([P, CHUNK], F32, tag="turn", name="spare")
-        for i in range(9):
+        for i in range(11):
             nc.tensor.matmul_mx(
                 out=spare[:],
                 lhsT=w_codes[:].bitcast(FP8X4),
@@ -185,8 +181,8 @@ def tile_graphconvolutionbatch_s_kernel(tc, H, W, gamma, beta, out):
                 stop=True,
             )
 
-        def keep_busy(values):
-            nc.tensor.matmul(out=spare[:, 0:P], lhsT=zeros[:], rhs=values, start=True, stop=True)
+        def keep_clock_up():
+            nc.tensor.matmul(out=spare[:, 0:P], lhsT=zeros[:], rhs=zeros[:], start=True, stop=True)
 
         gamma_d = keep.tile([P, 3], F32)
         minus_gamma_d = keep.tile([P, 3], F32)
@@ -319,10 +315,8 @@ def tile_graphconvolutionbatch_s_kernel(tc, H, W, gamma, beta, out):
         BEHIND = 2
         for unit in relu_units[:AHEAD]:
             relu(*unit)
-        keep_busy(x[0][:, 1:5, EVEN : EVEN + COLS])
         sum_pairs(*sum_units[0])
         sum_pairs(*sum_units[1])
-        keep_busy(pair[:, 0, 0:8, :])
         for i in range(len(sum_units)):
             if i + AHEAD < len(relu_units):
                 relu(*relu_units[i + AHEAD])
@@ -334,6 +328,8 @@ def tile_graphconvolutionbatch_s_kernel(tc, H, W, gamma, beta, out):
             g = i - 1
             if g >= 0:
                 sum_rows(g)
+                if g < 6:
+                    keep_clock_up()
             if g >= BEHIND:
                 store(g - BEHIND)
         for g in range(GROUPS - BEHIND, GROUPS):

@@ -36,6 +36,8 @@ X_WIDTH = 44
 
 VECTOR_COPIES = (1,)
 
+CLOCK_GROUPS = (0, 1, 3, 4, 6)
+
 TOP, MIDDLE, BOTTOM = 0, 1, 2
 
 
@@ -72,8 +74,6 @@ def tile_graphconvolutionbatch_s_kernel(tc, H, W, gamma, beta, out):
         nc.sync.dma_start(out=gamma_bf[:], in_=gamma.rearrange("(p o) -> p o", o=1))
         nc.sync.dma_start(out=beta_bf[:], in_=beta.rearrange("(p o) -> p o", o=1))
 
-        zeros = keep.tile([P, P], F32)
-        nc.vector.memset(zeros[:], 0.0)
         ident = keep.tile([P, P], F32)
         make_identity(nc, ident[:])
         eps_bn = keep.tile([P, 1], F32)
@@ -162,11 +162,11 @@ def tile_graphconvolutionbatch_s_kernel(tc, H, W, gamma, beta, out):
             turn(g)
             if g > 0:
                 quantise(g - 1)
-            if g in (4, 6):
-                multiply(g // 2 - 2)
-                take_statistics(g // 2 - 2)
+            if g == 4:
+                multiply(0)
+                take_statistics(0)
         quantise(GROUPS - 1)
-        for j in (2, 3):
+        for j in (1, 2, 3):
             multiply(j)
             take_statistics(j)
         spare = psum.tile([P, CHUNK], F32, tag="turn", name="spare")
@@ -180,9 +180,6 @@ def tile_graphconvolutionbatch_s_kernel(tc, H, W, gamma, beta, out):
                 start=True,
                 stop=True,
             )
-
-        def keep_clock_up():
-            nc.tensor.matmul(out=spare[:, 0:P], lhsT=zeros[:], rhs=zeros[:], start=True, stop=True)
 
         gamma_d = keep.tile([P, 3], F32)
         minus_gamma_d = keep.tile([P, 3], F32)
@@ -281,7 +278,7 @@ def tile_graphconvolutionbatch_s_kernel(tc, H, W, gamma, beta, out):
                         out=boxes[g][par],
                         lhsT=col_sums[b][:, 1 - par, top + dr : top + dr + GROUP_ROWS, :].rearrange("f r m -> f (r m)"),
                         rhs=ident[:],
-                        is_transpose=True,
+                        is_transpose=not (g in CLOCK_GROUPS and par == dr == 0),
                         start=(dr == 0),
                         stop=(dr == 2),
                     )
@@ -328,8 +325,6 @@ def tile_graphconvolutionbatch_s_kernel(tc, H, W, gamma, beta, out):
             g = i - 1
             if g >= 0:
                 sum_rows(g)
-                if g < 6:
-                    keep_clock_up()
             if g >= BEHIND:
                 store(g - BEHIND)
         for g in range(GROUPS - BEHIND, GROUPS):

@@ -162,11 +162,11 @@ def tile_graphconvolutionbatch_s_kernel(tc, H, W, gamma, beta, out):
             turn(g)
             if g > 0:
                 quantise(g - 1)
-            if g == 4:
-                multiply(0)
-                take_statistics(0)
+            if g in (4, 6):
+                multiply(g // 2 - 2)
+                take_statistics(g // 2 - 2)
         quantise(GROUPS - 1)
-        for j in (1, 2, 3):
+        for j in (2, 3):
             multiply(j)
             take_statistics(j)
         spare = psum.tile([P, CHUNK], F32, tag="turn", name="spare")
@@ -181,26 +181,29 @@ def tile_graphconvolutionbatch_s_kernel(tc, H, W, gamma, beta, out):
                 stop=True,
             )
 
-        gamma_d = keep.tile([P, 3], F32)
         minus_gamma_d = keep.tile([P, 3], F32)
-        beta_d = keep.tile([P, 3], F32)
+        factor = keep.tile([P, 2, 8], F32)
+        term = keep.tile([P, 2, 8], F32)
+        nc.gpsimd.memset(term[:], 0.0)
         for kind in (INSIDE, EDGE, CORNER):
             one = slice(kind, kind + 1)
-            nc.gpsimd.tensor_scalar_mul(out=gamma_d[:, one], in0=gamma_bf[:], scalar1=D_KINDS[kind])
+            nc.gpsimd.tensor_scalar_mul(out=factor[:, 0, one], in0=gamma_bf[:], scalar1=D_KINDS[kind])
             nc.gpsimd.tensor_scalar_mul(out=minus_gamma_d[:, one], in0=gamma_bf[:], scalar1=-D_KINDS[kind])
-            nc.gpsimd.tensor_scalar_mul(out=beta_d[:, one], in0=beta_bf[:], scalar1=D_KINDS[kind])
+            nc.gpsimd.tensor_scalar_mul(out=term[:, 1, one], in0=beta_bf[:], scalar1=D_KINDS[kind])
 
         mean_var = keep.tile([P, 2], F32)
         nc.vector.bn_aggr(out=mean_var[:], in_=stats[:].rearrange("f j s -> f (j s)"))
         rstd = keep.tile([P, 1], F32)
-        minus_mean_gamma_d = keep.tile([P, 3], F32)
-        scale = keep.tile([P, 3], F32)
-        bias = keep.tile([P, 3], F32)
+        scale_bias = keep.tile([P, 2, 8], F32)
         nc.scalar.activation(out=rstd[:], in_=mean_var[:, 1:2], func=ACT.Abs_reciprocal_sqrt, bias=eps_bn[:])
-        nc.vector.tensor_scalar_mul(out=minus_mean_gamma_d[:], in0=minus_gamma_d[:], scalar1=mean_var[:, 0:1])
-        nc.vector.tensor_scalar_mul(out=scale[:], in0=gamma_d[:], scalar1=rstd[:])
+        nc.vector.tensor_scalar_mul(out=factor[:, 1, 0:3], in0=minus_gamma_d[:], scalar1=mean_var[:, 0:1])
         nc.vector.scalar_tensor_tensor(
-            out=bias[:], in0=minus_mean_gamma_d[:], scalar=rstd[:], in1=beta_d[:], op0=ALU.mult, op1=ALU.add
+            out=scale_bias[:, :, 0:3],
+            in0=factor[:, :, 0:3],
+            scalar=rstd[:],
+            in1=term[:, :, 0:3],
+            op0=ALU.mult,
+            op1=ALU.add,
         )
 
         def relu_inner(b, rows, kind):
@@ -212,8 +215,8 @@ def tile_graphconvolutionbatch_s_kernel(tc, H, W, gamma, beta, out):
                 out=x[b][:, rows, EVEN + 1 : EVEN + 1 + 2 * step].rearrange("f r (t s) -> f r t s", t=2)[:, :, :, 0:run],
                 in_=y_rows[:, :, 1 : 1 + 2 * run].rearrange("f r (t m) -> f r t m", t=2),
                 func=ACT.Relu,
-                scale=scale[:, kind : kind + 1],
-                bias=bias[:, kind : kind + 1],
+                scale=scale_bias[:, 0, kind : kind + 1],
+                bias=scale_bias[:, 1, kind : kind + 1],
             )
 
         def relu_outer(b, rows, kind):
@@ -224,8 +227,8 @@ def tile_graphconvolutionbatch_s_kernel(tc, H, W, gamma, beta, out):
                 out=x[b][:, rows, EVEN : last + 1 : last - EVEN],
                 in_=y_rows[:, :, 0 : COLS : COLS - 1],
                 func=ACT.Relu,
-                scale=scale[:, kind : kind + 1],
-                bias=bias[:, kind : kind + 1],
+                scale=scale_bias[:, 0, kind : kind + 1],
+                bias=scale_bias[:, 1, kind : kind + 1],
             )
 
         outer_done = []

@@ -36,7 +36,7 @@ X_WIDTH = 44
 
 VECTOR_COPIES = (1,)
 
-CLOCK_GROUPS = (0, 1, 3, 4, 6)
+CLOCK_GROUPS = (0, 1, 3, 4)
 
 TOP, MIDDLE, BOTTOM = 0, 1, 2
 
@@ -166,20 +166,29 @@ def tile_graphconvolutionbatch_s_kernel(tc, H, W, gamma, beta, out):
                 multiply(g // 2 - 2)
                 take_statistics(g // 2 - 2)
         quantise(GROUPS - 1)
-        for j in (2, 3):
-            multiply(j)
-            take_statistics(j)
         spare = psum.tile([P, CHUNK], F32, tag="turn", name="spare")
-        for i in range(11):
+
+        def multiply_again(j):
             nc.tensor.matmul_mx(
                 out=spare[:],
                 lhsT=w_codes[:].bitcast(FP8X4),
                 lhsT_scale=w_scales[:],
-                rhs=h_codes[:, NODES - CHUNK :].bitcast(FP8X4),
-                rhs_scale=h_scales[:, NODES - CHUNK :],
+                rhs=h_codes[:, j * CHUNK : (j + 1) * CHUNK].bitcast(FP8X4),
+                rhs_scale=h_scales[:, j * CHUNK : (j + 1) * CHUNK],
                 start=True,
                 stop=True,
             )
+
+        def multiply_identity(values):
+            nc.tensor.matmul(out=spare[:, 0:P], lhsT=ident[:], rhs=values, start=True, stop=True)
+
+        multiply(2)
+        take_statistics(2)
+        multiply_again(2)
+        multiply(3)
+        take_statistics(3)
+        for i in range(7):
+            multiply_again(3)
 
         minus_gamma_d = keep.tile([P, 3], F32)
         factor = keep.tile([P, 2, 8], F32)
@@ -269,7 +278,8 @@ def tile_graphconvolutionbatch_s_kernel(tc, H, W, gamma, beta, out):
             b = g // GROUPS_PER_IMAGE
             top = (g % GROUPS_PER_IMAGE) * GROUP_ROWS
             if g < GROUPS - 1:
-                both = psum.tile([P, 2, OUT_DIM], F32, tag="turn", name="box%d" % g)[:]
+                tag = "turn" if g % 2 == 0 else "product"
+                both = psum.tile([P, 2, OUT_DIM], F32, tag=tag, name="box%d" % g)[:]
                 boxes.append((both[:, 0, :], both[:, 1, :], both))
             else:
                 even = psum.tile([P, OUT_DIM], F32, tag="turn", name="box_even")
@@ -312,11 +322,13 @@ def tile_graphconvolutionbatch_s_kernel(tc, H, W, gamma, beta, out):
         relu_units = [(0, 0, 5), (0, 5, 9)] + relu_units[1:]
         sum_units = [(0, 0, 5), (0, 5, 9)] + sum_units[1:]
         AHEAD = 4
-        BEHIND = 2
+        BEHIND = 3
         for unit in relu_units[:AHEAD]:
             relu(*unit)
+        multiply_identity(x[0][:, 1:5, EVEN : EVEN + COLS])
         sum_pairs(*sum_units[0])
         sum_pairs(*sum_units[1])
+        multiply_identity(pair[:, 0, 0:8, :])
         for i in range(len(sum_units)):
             if i + AHEAD < len(relu_units):
                 relu(*relu_units[i + AHEAD])

@@ -17,6 +17,8 @@ EPS_DEG = 1e-5
 
 FLOPS = 2 * NODES * IN_DIM * OUT_DIM
 
+Y_BANKS = 4
+TURN_BANKS = 8 - Y_BANKS
 HALF_COLS = COLS // 2
 GROUP = 2 * P
 GROUPS = NODES // GROUP
@@ -34,7 +36,7 @@ EVEN = 4
 ODD = 24
 X_WIDTH = 44
 
-VECTOR_COPIES = (1,)
+VECTOR_COPIES = ()
 
 CLOCK_GROUPS = (0, 1, 3, 4)
 
@@ -60,15 +62,16 @@ def tile_graphconvolutionbatch_s_kernel(tc, H, W, gamma, beta, out):
         tc.manual_schedule(),
     ):
         w_raw = keep.tile([P, 4, OUT_DIM], BF16)
-        nc.scalar.dma_start(
-            out=w_raw[:].rearrange("q t c -> q (t c)"), in_=W.rearrange("(q t) c -> q (t c)", t=4)
-        )
         h_sb = keep.tile([P, GROUPS, 2 * IN_DIM], BF16)
         for g in range(GROUPS):
             nc.sync.dma_start(
                 out=h_sb[:, g, :],
                 in_=h_rows[g * GROUP : (g + 1) * GROUP, :].rearrange("(p t) k -> p (t k)", t=2),
             )
+            if g == 0:
+                nc.sync.dma_start(
+                    out=w_raw[:].rearrange("q t c -> q (t c)"), in_=W.rearrange("(q t) c -> q (t c)", t=4)
+                )
         gamma_bf = keep.tile([P, 1], BF16)
         beta_bf = keep.tile([P, 1], BF16)
         nc.sync.dma_start(out=gamma_bf[:], in_=gamma.rearrange("(p o) -> p o", o=1))
@@ -122,11 +125,12 @@ def tile_graphconvolutionbatch_s_kernel(tc, H, W, gamma, beta, out):
         h_grouped_words = h_grouped[:].bitcast(F32).rearrange("q (n u) -> q n u", u=2)
         h_codes = keep.tile([P, NODES], U32, align_bytes=64)
         h_scales = keep.tile([P, NODES], U8, align_bytes=64)
-        stats = keep.tile([P, CHUNKS, 6], F32)
+        passes = [(j * CHUNK, (j + 1) * CHUNK) for j in range(CHUNKS)]
+        stats = keep.tile([P, len(passes), 6], F32)
         y = []
 
         def turn(g):
-            h_t = psum.tile([P, 2, GROUP_ROWS, 2, HALF_COLS], F32, tag="turn")
+            h_t = psum.tile([P, 2, GROUP_ROWS, 2, HALF_COLS], F32, tag="turn", bufs=TURN_BANKS)
             for t in range(2):
                 for u in range(2):
                     nc.tensor.transpose(h_t[:, u, :, t, :], h_words[:, g, t, u, :], ident[:])
@@ -144,19 +148,29 @@ def tile_graphconvolutionbatch_s_kernel(tc, H, W, gamma, beta, out):
             )
 
         def multiply(j):
-            y.append(psum.tile([P, CHUNK_ROWS, COLS], F32, tag="product", name="y%d" % j))
+            first, end = passes[j]
+            y.append(psum.tile([P, (end - first) // COLS, COLS], F32, tag="product", bufs=Y_BANKS, name="y%d" % j))
             nc.tensor.matmul_mx(
                 out=y[j][:].rearrange("f r c -> f (r c)"),
                 lhsT=w_codes[:].bitcast(FP8X4),
                 lhsT_scale=w_scales[:],
-                rhs=h_codes[:, j * CHUNK : (j + 1) * CHUNK].bitcast(FP8X4),
-                rhs_scale=h_scales[:, j * CHUNK : (j + 1) * CHUNK],
+                rhs=h_codes[:, first:end].bitcast(FP8X4),
+                rhs_scale=h_scales[:, first:end],
                 start=True,
                 stop=True,
             )
 
         def take_statistics(j):
             nc.vector.bn_stats(out=stats[:, j, :], in_=y[j][:].rearrange("f r c -> f (r c)"))
+
+        def bank_of(b, row):
+            node = (b * ROWS + row) * COLS
+            return [j for j, (first, end) in enumerate(passes) if first <= node < end][0]
+
+        def y_rows(b, rows):
+            j = bank_of(b, rows.start)
+            first = b * ROWS + rows.start - passes[j][0] // COLS
+            return y[j][:, first : first + rows.stop - rows.start, :]
 
         for g in range(GROUPS):
             turn(g)
@@ -166,7 +180,7 @@ def tile_graphconvolutionbatch_s_kernel(tc, H, W, gamma, beta, out):
                 multiply(g // 2 - 2)
                 take_statistics(g // 2 - 2)
         quantise(GROUPS - 1)
-        spare = psum.tile([P, CHUNK], F32, tag="turn", name="spare")
+        spare = psum.tile([P, CHUNK], F32, tag="turn", bufs=TURN_BANKS, name="spare")
 
         def multiply_again(j):
             nc.tensor.matmul_mx(
@@ -215,61 +229,79 @@ def tile_graphconvolutionbatch_s_kernel(tc, H, W, gamma, beta, out):
             op1=ALU.add,
         )
 
-        def relu_inner(b, rows, kind):
-            run = HALF_COLS - 1
-            step = ODD - EVEN - 1
-            chunk, first = divmod(b * ROWS + rows.start, CHUNK_ROWS)
-            y_rows = y[chunk][:, first : first + rows.stop - rows.start, :]
+        def affine_even(b, first, end):
+            rows = slice(max(first, 1), min(end, ROWS - 1))
+            nc.vector.tensor_scalar(
+                out=x[b][:, rows, EVEN + 1 : EVEN + HALF_COLS],
+                in0=y_rows(b, rows)[:, :, 1:HALF_COLS],
+                scalar1=scale_bias[:, 0, INSIDE : INSIDE + 1],
+                scalar2=scale_bias[:, 1, INSIDE : INSIDE + 1],
+                op0=ALU.mult,
+                op1=ALU.add,
+            )
+
+        def relu_call(b, rows, columns, kind):
+            x_columns, y_columns = columns
+            out, in_ = x[b][:, rows, x_columns], y_rows(b, rows)[:, :, y_columns]
+            if columns == INNER:
+                out = out.rearrange("f r (t s) -> f r t s", t=2)[:, :, :, 0 : HALF_COLS - 1]
+                in_ = in_.rearrange("f r (t m) -> f r t m", t=2)
             nc.scalar.activation(
-                out=x[b][:, rows, EVEN + 1 : EVEN + 1 + 2 * step].rearrange("f r (t s) -> f r t s", t=2)[:, :, :, 0:run],
-                in_=y_rows[:, :, 1 : 1 + 2 * run].rearrange("f r (t m) -> f r t m", t=2),
+                out=out,
+                in_=in_,
                 func=ACT.Relu,
                 scale=scale_bias[:, 0, kind : kind + 1],
                 bias=scale_bias[:, 1, kind : kind + 1],
             )
 
-        def relu_outer(b, rows, kind):
-            chunk, first = divmod(b * ROWS + rows.start, CHUNK_ROWS)
-            y_rows = y[chunk][:, first : first + rows.stop - rows.start, :]
-            last = ODD + HALF_COLS - 1
-            nc.scalar.activation(
-                out=x[b][:, rows, EVEN : last + 1 : last - EVEN],
-                in_=y_rows[:, :, 0 : COLS : COLS - 1],
-                func=ACT.Relu,
-                scale=scale_bias[:, 0, kind : kind + 1],
-                bias=scale_bias[:, 1, kind : kind + 1],
-            )
-
-        outer_done = []
+        STEP = ODD - EVEN - 1
+        LAST = ODD + HALF_COLS - 1
+        INNER = (slice(EVEN + 1, EVEN + 1 + 2 * STEP), slice(1, COLS - 1))
+        INNER_ODD = (slice(ODD, LAST), slice(HALF_COLS, COLS - 1))
+        OUTER = (slice(EVEN, LAST + 1, LAST - EVEN), slice(0, COLS, COLS - 1))
+        VECTOR_ROWS = ((0,16,32,),(1,0,16,),)
+        OUTER_UNITS = ((0, 0, 5), (0, 5, 16), (0, 16, 32), (1, 0, 16), (1, 16, 32))
 
         def relu(b, first, end):
-            relu_inner(b, slice(max(first, 1), min(end, ROWS - 1)), INSIDE)
-            bank = (first // CHUNK_ROWS) * CHUNK_ROWS
-            if (b, bank) not in outer_done:
-                outer_done.append((b, bank))
-                relu_outer(b, slice(max(bank, 1), min(bank + CHUNK_ROWS, ROWS - 1)), EDGE)
+            halved = any(image == b and start <= first and end <= stop for image, start, stop in VECTOR_ROWS)
+            relu_call(b, slice(max(first, 1), min(end, ROWS - 1)), INNER_ODD if halved else INNER, INSIDE)
+            for image, start, stop in OUTER_UNITS:
+                if image == b and start == first:
+                    relu_call(b, slice(max(start, 1), min(stop, ROWS - 1)), OUTER, EDGE)
             for row in (0, ROWS - 1):
                 if first <= row < end:
-                    relu_inner(b, slice(row, row + 1), EDGE)
-                    relu_outer(b, slice(row, row + 1), CORNER)
+                    relu_call(b, slice(row, row + 1), INNER, EDGE)
+                    relu_call(b, slice(row, row + 1), OUTER, CORNER)
 
         pair = keep.tile([P, BATCH, ROWS, HALF_COLS], F32)
 
         def sum_pairs(b, first, end):
             rows = slice(first, end)
-            nc.vector.tensor_add(
-                out=pair[:, b, rows, :], in0=x[b][:, rows, ODD : ODD + HALF_COLS], in1=x[b][:, rows, EVEN : EVEN + HALF_COLS]
+            nc.vector.scalar_tensor_tensor(
+                out=pair[:, b, rows, :],
+                in0=x[b][:, rows, EVEN : EVEN + HALF_COLS],
+                scalar=0.0,
+                in1=x[b][:, rows, ODD : ODD + HALF_COLS],
+                op0=ALU.max,
+                op1=ALU.add,
             )
 
         def sum_columns(b, first, end):
             rows = slice(first, end)
             step = ODD - EVEN - 2
             third = x[b][:, rows, EVEN + 1 : EVEN + 1 + 2 * step].rearrange("f r (a s) -> f a r s", a=2)
-            nc.vector.tensor_add(
-                out=col_sums[b][:, :, 1 + first : 1 + end, :],
-                in0=pair[:, b, rows, :].unsqueeze(1).to_broadcast([P, 2, end - first, HALF_COLS]),
-                in1=third[:, :, :, 0:HALF_COLS],
-            )
+            sums, pairs = col_sums[b][:, :, 1 + first : 1 + end, :], pair[:, b, rows, :]
+            if any(image == b and first < stop and end > start for image, start, stop in VECTOR_ROWS):
+                nc.vector.scalar_tensor_tensor(
+                    out=sums[:, 0, :, :], in0=third[:, 0, :, 0:HALF_COLS], scalar=0.0, in1=pairs, op0=ALU.max, op1=ALU.add
+                )
+                nc.vector.tensor_add(out=sums[:, 1, :, :], in0=pairs, in1=third[:, 1, :, 0:HALF_COLS])
+            else:
+                nc.vector.tensor_add(
+                    out=sums,
+                    in0=pairs.unsqueeze(1).to_broadcast([P, 2, end - first, HALF_COLS]),
+                    in1=third[:, :, :, 0:HALF_COLS],
+                )
 
         out_sb = keep.tile([P, GROUPS, 2, OUT_DIM], F32)
         boxes = []
@@ -279,11 +311,11 @@ def tile_graphconvolutionbatch_s_kernel(tc, H, W, gamma, beta, out):
             top = (g % GROUPS_PER_IMAGE) * GROUP_ROWS
             if g < GROUPS - 1:
                 tag = "turn" if g % 2 == 0 else "product"
-                both = psum.tile([P, 2, OUT_DIM], F32, tag=tag, name="box%d" % g)[:]
+                both = psum.tile([P, 2, OUT_DIM], F32, tag=tag, bufs=TURN_BANKS if tag == "turn" else Y_BANKS, name="box%d" % g)[:]
                 boxes.append((both[:, 0, :], both[:, 1, :], both))
             else:
-                even = psum.tile([P, OUT_DIM], F32, tag="turn", name="box_even")
-                odd = psum.tile([P, OUT_DIM], F32, tag="product", name="box_odd")
+                even = psum.tile([P, OUT_DIM], F32, tag="turn", bufs=TURN_BANKS, name="box_even")
+                odd = psum.tile([P, OUT_DIM], F32, tag="product", bufs=Y_BANKS, name="box_odd")
                 boxes.append((even[:], odd[:], None))
             for par in range(2):
                 for dr in range(3):
@@ -306,7 +338,7 @@ def tile_graphconvolutionbatch_s_kernel(tc, H, W, gamma, beta, out):
             if g == GROUPS - 1:
                 scaled_on_scalar(0, even)
                 nc.vector.tensor_scalar_mul(out=out_sb[:, g, 1, :], in0=odd, scalar1=d[:, 1:2])
-            elif g in (1, 4):
+            elif g in (0, 1, 2, 3):
                 scaled_on_scalar(0, even)
                 scaled_on_scalar(1, odd)
             else:
@@ -315,14 +347,12 @@ def tile_graphconvolutionbatch_s_kernel(tc, H, W, gamma, beta, out):
                 )
             nc.sync.dma_start(out=out_groups[:, g, :], in_=out_sb[:, g, :, :].rearrange("p two f -> p (two f)"))
 
-        relu_rows = ((0, 9), (9, 16), (16, 25), (25, 32))
-        sum_rows_of_group = ((0, 9), (9, 17), (17, 25), (25, 32))
-        relu_units = [(b, first, end) for b in range(BATCH) for first, end in relu_rows]
-        sum_units = [(b, first, end) for b in range(BATCH) for first, end in sum_rows_of_group]
-        relu_units = [(0, 0, 5), (0, 5, 9)] + relu_units[1:]
-        sum_units = [(0, 0, 5), (0, 5, 9)] + sum_units[1:]
+        relu_units = [(0, 0, 5), (0, 5, 9), (0, 9, 16), (0, 16, 24), (0, 24, 32), (1, 0, 8), (1, 8, 16), (1, 16, 24), (1, 24, 32)]
+        sum_units = [(0, 0, 5), (0, 5, 9), (0, 9, 17), (0, 17, 25), (0, 25, 32), (1, 0, 9), (1, 9, 17), (1, 17, 25), (1, 25, 32)]
         AHEAD = 4
         BEHIND = 3
+        affine_even(0, 16, 32)
+        affine_even(1, 0, 16)
         for unit in relu_units[:AHEAD]:
             relu(*unit)
         multiply_identity(x[0][:, 1:5, EVEN : EVEN + COLS])

@@ -4,6 +4,7 @@ from concourse.masks import make_identity
 F32 = mybir.dt.float32
 BF16 = mybir.dt.bfloat16
 U32 = mybir.dt.uint32
+I32 = mybir.dt.int32
 U8 = mybir.dt.uint8
 FP8X4 = mybir.dt.float8_e4m3fn_x4
 ACT = mybir.ActivationFunctionType
@@ -193,8 +194,10 @@ def tile_graphconvolutionbatch_s_kernel(tc, H, W, gamma, beta, out):
                 stop=True,
             )
 
-        def multiply_identity(values):
-            nc.tensor.matmul(out=spare[:, 0:P], lhsT=ident[:], rhs=values, start=True, stop=True)
+        def multiply_again_behind_vector(j):
+            words = h_codes[:, j * CHUNK : j * CHUNK + 16].bitcast(I32)
+            nc.vector.tensor_copy(out=words, in_=words)
+            multiply_again(j)
 
         multiply(2)
         take_statistics(2)
@@ -352,13 +355,14 @@ def tile_graphconvolutionbatch_s_kernel(tc, H, W, gamma, beta, out):
         AHEAD = 4
         BEHIND = 3
         affine_even(0, 16, 32)
+        multiply_again_behind_vector(0)
         affine_even(1, 0, 16)
+        multiply_again_behind_vector(1)
         for unit in relu_units[:AHEAD]:
             relu(*unit)
-        multiply_identity(x[0][:, 1:5, EVEN : EVEN + COLS])
         sum_pairs(*sum_units[0])
         sum_pairs(*sum_units[1])
-        multiply_identity(pair[:, 0, 0:8, :])
+        multiply_again_behind_vector(2)
         for i in range(len(sum_units)):
             if i + AHEAD < len(relu_units):
                 relu(*relu_units[i + AHEAD])

import concourse.mybir as mybir
from concourse.masks import make_identity

F32 = mybir.dt.float32
BF16 = mybir.dt.bfloat16
U32 = mybir.dt.uint32
I32 = mybir.dt.int32
U8 = mybir.dt.uint8
FP8X4 = mybir.dt.float8_e4m3fn_x4
ACT = mybir.ActivationFunctionType
ALU = mybir.AluOpType

P = 128
BATCH, ROWS, COLS, IN_DIM, OUT_DIM = 2, 32, 32, 512, 128
NODES = BATCH * ROWS * COLS
EPS_BN = 1e-5
EPS_DEG = 1e-5

FLOPS = 2 * NODES * IN_DIM * OUT_DIM

Y_BANKS = 4
TURN_BANKS = 8 - Y_BANKS
HALF_COLS = COLS // 2
GROUP = 2 * P
GROUPS = NODES // GROUP
GROUP_ROWS = GROUP // COLS
GROUPS_PER_IMAGE = GROUPS // BATCH
CHUNK = 2 * GROUP
CHUNKS = NODES // CHUNK
CHUNK_ROWS = CHUNK // COLS
WORDS = IN_DIM // 2

D_KINDS = ((9 + EPS_DEG) ** -0.5, (6 + EPS_DEG) ** -0.5, (4 + EPS_DEG) ** -0.5)
INSIDE, EDGE, CORNER = 0, 1, 2

EVEN = 4
ODD = 24
X_WIDTH = 44

VECTOR_COPIES = ()

CLOCK_GROUPS = (0, 1, 3, 4)

TOP, MIDDLE, BOTTOM = 0, 1, 2


def group_kind(g):
    if g % GROUPS_PER_IMAGE == 0:
        return TOP
    if g % GROUPS_PER_IMAGE == GROUPS_PER_IMAGE - 1:
        return BOTTOM
    return MIDDLE


def tile_graphconvolutionbatch_s_kernel(tc, H, W, gamma, beta, out):
    nc = tc.nc
    h_rows = H.flatten_outer_dims()
    out_groups = out.flatten_outer_dims().rearrange("(g p two) f -> p g (two f)", p=P, two=2)

    with (
        tc.tile_pool(name="keep", bufs=1) as keep,
        tc.psum_pool(name="psum", bufs=4) as psum,
        tc.manual_schedule(),
    ):
        w_raw = keep.tile([P, 4, OUT_DIM], BF16)
        h_sb = keep.tile([P, GROUPS, 2 * IN_DIM], BF16)
        for g in range(GROUPS):
            nc.sync.dma_start(
                out=h_sb[:, g, :],
                in_=h_rows[g * GROUP : (g + 1) * GROUP, :].rearrange("(p t) k -> p (t k)", t=2),
            )
            if g == 0:
                nc.sync.dma_start(
                    out=w_raw[:].rearrange("q t c -> q (t c)"), in_=W.rearrange("(q t) c -> q (t c)", t=4)
                )
        gamma_bf = keep.tile([P, 1], BF16)
        beta_bf = keep.tile([P, 1], BF16)
        nc.sync.dma_start(out=gamma_bf[:], in_=gamma.rearrange("(p o) -> p o", o=1))
        nc.sync.dma_start(out=beta_bf[:], in_=beta.rearrange("(p o) -> p o", o=1))

        ident = keep.tile([P, P], F32)
        make_identity(nc, ident[:])
        eps_bn = keep.tile([P, 1], F32)
        eps_deg = keep.tile([P, 1], F32)
        nc.vector.memset(eps_bn[:], EPS_BN)
        nc.vector.memset(eps_deg[:], EPS_DEG)
        table_warm = keep.tile([P, 1], F32)
        nc.scalar.activation(out=table_warm[:], in_=eps_bn[:], func=ACT.Abs_reciprocal_sqrt)

        border = keep.tile([P, 5], F32)
        nc.vector.memset(border[:], 0.0)
        first_row, last_row = slice(0, HALF_COLS), slice(P - HALF_COLS, P)
        for column, members in enumerate(
            (slice(0, P, HALF_COLS), slice(HALF_COLS - 1, P, HALF_COLS), first_row, None, last_row)
        ):
            if members is not None:
                nc.vector.reduce_sum(
                    out=border[:, column : column + 1], in_=ident[:, members], axis=mybir.AxisListType.X
                )
        nc.vector.tensor_scalar(out=border[:], in0=border[:], scalar1=-1.0, scalar2=3.0, op0=ALU.mult, op1=ALU.add)
        degree = keep.tile([P, 3, 2], F32)
        nc.vector.tensor_mul(
            out=degree[:],
            in0=border[:, 2:5].unsqueeze(2).to_broadcast([P, 3, 2]),
            in1=border[:, 0:2].unsqueeze(1).to_broadcast([P, 3, 2]),
        )
        d_out = keep.tile([P, 3, 2], F32)
        nc.scalar.activation(out=d_out[:], in_=degree[:], func=ACT.Abs_reciprocal_sqrt, bias=eps_deg[:])

        x = [keep.tile([P, ROWS, X_WIDTH], F32, name="x%d" % b) for b in range(BATCH)]
        col_sums = [keep.tile([P, 2, ROWS + 2, HALF_COLS], F32, name="col_sums%d" % b) for b in range(BATCH)]
        for b in range(BATCH):
            nc.gpsimd.memset(x[b][:, :, EVEN + HALF_COLS : ODD], 0.0)
            nc.gpsimd.memset(col_sums[b][:, :, 0 : ROWS + 2 : ROWS + 1, :], 0.0)

        w_grouped = keep.tile([P, OUT_DIM, 4], BF16, align_bytes=64)
        w_codes = keep.tile([P, OUT_DIM], U32, align_bytes=64)
        w_scales = keep.tile([P, OUT_DIM], U8, align_bytes=64)
        nc.vector.tensor_copy(out=w_grouped[:], in_=w_raw[:].rearrange("q t c -> q c t"))
        nc.vector.quantize_mx(
            out=w_codes[:].bitcast(FP8X4), scales=w_scales[:], in_=w_grouped[:].rearrange("q c t -> q (c t)")
        )

        h_words = h_sb[:].bitcast(F32).rearrange("p g (t w u) -> p g t u w", t=2, u=2)
        h_grouped = keep.tile([P, NODES * 4], BF16, align_bytes=64)
        h_grouped_words = h_grouped[:].bitcast(F32).rearrange("q (n u) -> q n u", u=2)
        h_codes = keep.tile([P, NODES], U32, align_bytes=64)
        h_scales = keep.tile([P, NODES], U8, align_bytes=64)
        passes = [(j * CHUNK, (j + 1) * CHUNK) for j in range(CHUNKS)]
        stats = keep.tile([P, len(passes), 6], F32)
        y = []

        def turn(g):
            h_t = psum.tile([P, 2, GROUP_ROWS, 2, HALF_COLS], F32, tag="turn", bufs=TURN_BANKS)
            for t in range(2):
                for u in range(2):
                    nc.tensor.transpose(h_t[:, u, :, t, :], h_words[:, g, t, u, :], ident[:])
            copy = nc.vector.tensor_copy if g in VECTOR_COPIES else nc.scalar.copy
            copy(
                out=h_grouped_words[:, g * GROUP : (g + 1) * GROUP, :],
                in_=h_t[:].rearrange("q u r t m -> q (r t m) u"),
            )

        def quantise(g):
            nc.vector.quantize_mx(
                out=h_codes[:, g * GROUP : (g + 1) * GROUP].bitcast(FP8X4),
                scales=h_scales[:, g * GROUP : (g + 1) * GROUP],
                in_=h_grouped[:, 4 * g * GROUP : 4 * (g + 1) * GROUP],
            )

        def multiply(j):
            first, end = passes[j]
            y.append(psum.tile([P, (end - first) // COLS, COLS], F32, tag="product", bufs=Y_BANKS, name="y%d" % j))
            nc.tensor.matmul_mx(
                out=y[j][:].rearrange("f r c -> f (r c)"),
                lhsT=w_codes[:].bitcast(FP8X4),
                lhsT_scale=w_scales[:],
                rhs=h_codes[:, first:end].bitcast(FP8X4),
                rhs_scale=h_scales[:, first:end],
                start=True,
                stop=True,
            )

        def take_statistics(j):
            nc.vector.bn_stats(out=stats[:, j, :], in_=y[j][:].rearrange("f r c -> f (r c)"))

        def bank_of(b, row):
            node = (b * ROWS + row) * COLS
            return [j for j, (first, end) in enumerate(passes) if first <= node < end][0]

        def y_rows(b, rows):
            j = bank_of(b, rows.start)
            first = b * ROWS + rows.start - passes[j][0] // COLS
            return y[j][:, first : first + rows.stop - rows.start, :]

        for g in range(GROUPS):
            turn(g)
            if g > 0:
                quantise(g - 1)
            if g in (4, 6):
                multiply(g // 2 - 2)
                take_statistics(g // 2 - 2)
        quantise(GROUPS - 1)
        spare = psum.tile([P, CHUNK], F32, tag="turn", bufs=TURN_BANKS, name="spare")

        def multiply_again(j):
            nc.tensor.matmul_mx(
                out=spare[:],
                lhsT=w_codes[:].bitcast(FP8X4),
                lhsT_scale=w_scales[:],
                rhs=h_codes[:, j * CHUNK : (j + 1) * CHUNK].bitcast(FP8X4),
                rhs_scale=h_scales[:, j * CHUNK : (j + 1) * CHUNK],
                start=True,
                stop=True,
            )

        def multiply_again_behind_vector(j):
            words = h_codes[:, j * CHUNK : j * CHUNK + 16].bitcast(I32)
            nc.vector.tensor_copy(out=words, in_=words)
            multiply_again(j)

        multiply(2)
        take_statistics(2)
        multiply_again(2)
        multiply(3)
        take_statistics(3)
        for i in range(7):
            multiply_again(3)

        minus_gamma_d = keep.tile([P, 3], F32)
        factor = keep.tile([P, 2, 8], F32)
        term = keep.tile([P, 2, 8], F32)
        nc.gpsimd.memset(term[:], 0.0)
        for kind in (INSIDE, EDGE, CORNER):
            one = slice(kind, kind + 1)
            nc.gpsimd.tensor_scalar_mul(out=factor[:, 0, one], in0=gamma_bf[:], scalar1=D_KINDS[kind])
            nc.gpsimd.tensor_scalar_mul(out=minus_gamma_d[:, one], in0=gamma_bf[:], scalar1=-D_KINDS[kind])
            nc.gpsimd.tensor_scalar_mul(out=term[:, 1, one], in0=beta_bf[:], scalar1=D_KINDS[kind])

        mean_var = keep.tile([P, 2], F32)
        nc.vector.bn_aggr(out=mean_var[:], in_=stats[:].rearrange("f j s -> f (j s)"))
        rstd = keep.tile([P, 1], F32)
        scale_bias = keep.tile([P, 2, 8], F32)
        nc.scalar.activation(out=rstd[:], in_=mean_var[:, 1:2], func=ACT.Abs_reciprocal_sqrt, bias=eps_bn[:])
        nc.vector.tensor_scalar_mul(out=factor[:, 1, 0:3], in0=minus_gamma_d[:], scalar1=mean_var[:, 0:1])
        nc.vector.scalar_tensor_tensor(
            out=scale_bias[:, :, 0:3],
            in0=factor[:, :, 0:3],
            scalar=rstd[:],
            in1=term[:, :, 0:3],
            op0=ALU.mult,
            op1=ALU.add,
        )

        def affine_even(b, first, end):
            rows = slice(max(first, 1), min(end, ROWS - 1))
            nc.vector.tensor_scalar(
                out=x[b][:, rows, EVEN + 1 : EVEN + HALF_COLS],
                in0=y_rows(b, rows)[:, :, 1:HALF_COLS],
                scalar1=scale_bias[:, 0, INSIDE : INSIDE + 1],
                scalar2=scale_bias[:, 1, INSIDE : INSIDE + 1],
                op0=ALU.mult,
                op1=ALU.add,
            )

        def relu_call(b, rows, columns, kind):
            x_columns, y_columns = columns
            out, in_ = x[b][:, rows, x_columns], y_rows(b, rows)[:, :, y_columns]
            if columns == INNER:
                out = out.rearrange("f r (t s) -> f r t s", t=2)[:, :, :, 0 : HALF_COLS - 1]
                in_ = in_.rearrange("f r (t m) -> f r t m", t=2)
            nc.scalar.activation(
                out=out,
                in_=in_,
                func=ACT.Relu,
                scale=scale_bias[:, 0, kind : kind + 1],
                bias=scale_bias[:, 1, kind : kind + 1],
            )

        STEP = ODD - EVEN - 1
        LAST = ODD + HALF_COLS - 1
        INNER = (slice(EVEN + 1, EVEN + 1 + 2 * STEP), slice(1, COLS - 1))
        INNER_ODD = (slice(ODD, LAST), slice(HALF_COLS, COLS - 1))
        OUTER = (slice(EVEN, LAST + 1, LAST - EVEN), slice(0, COLS, COLS - 1))
        VECTOR_ROWS = ((0,16,32,),(1,0,16,),)
        OUTER_UNITS = ((0, 0, 5), (0, 5, 16), (0, 16, 32), (1, 0, 16), (1, 16, 32))

        def relu(b, first, end):
            halved = any(image == b and start <= first and end <= stop for image, start, stop in VECTOR_ROWS)
            relu_call(b, slice(max(first, 1), min(end, ROWS - 1)), INNER_ODD if halved else INNER, INSIDE)
            for image, start, stop in OUTER_UNITS:
                if image == b and start == first:
                    relu_call(b, slice(max(start, 1), min(stop, ROWS - 1)), OUTER, EDGE)
            for row in (0, ROWS - 1):
                if first <= row < end:
                    relu_call(b, slice(row, row + 1), INNER, EDGE)
                    relu_call(b, slice(row, row + 1), OUTER, CORNER)

        pair = keep.tile([P, BATCH, ROWS, HALF_COLS], F32)

        def sum_pairs(b, first, end):
            rows = slice(first, end)
            nc.vector.scalar_tensor_tensor(
                out=pair[:, b, rows, :],
                in0=x[b][:, rows, EVEN : EVEN + HALF_COLS],
                scalar=0.0,
                in1=x[b][:, rows, ODD : ODD + HALF_COLS],
                op0=ALU.max,
                op1=ALU.add,
            )

        def sum_columns(b, first, end):
            rows = slice(first, end)
            step = ODD - EVEN - 2
            third = x[b][:, rows, EVEN + 1 : EVEN + 1 + 2 * step].rearrange("f r (a s) -> f a r s", a=2)
            sums, pairs = col_sums[b][:, :, 1 + first : 1 + end, :], pair[:, b, rows, :]
            if any(image == b and first < stop and end > start for image, start, stop in VECTOR_ROWS):
                nc.vector.scalar_tensor_tensor(
                    out=sums[:, 0, :, :], in0=third[:, 0, :, 0:HALF_COLS], scalar=0.0, in1=pairs, op0=ALU.max, op1=ALU.add
                )
                nc.vector.tensor_add(out=sums[:, 1, :, :], in0=pairs, in1=third[:, 1, :, 0:HALF_COLS])
            else:
                nc.vector.tensor_add(
                    out=sums,
                    in0=pairs.unsqueeze(1).to_broadcast([P, 2, end - first, HALF_COLS]),
                    in1=third[:, :, :, 0:HALF_COLS],
                )

        out_sb = keep.tile([P, GROUPS, 2, OUT_DIM], F32)
        boxes = []

        def sum_rows(g):
            b = g // GROUPS_PER_IMAGE
            top = (g % GROUPS_PER_IMAGE) * GROUP_ROWS
            if g < GROUPS - 1:
                tag = "turn" if g % 2 == 0 else "product"
                both = psum.tile([P, 2, OUT_DIM], F32, tag=tag, bufs=TURN_BANKS if tag == "turn" else Y_BANKS, name="box%d" % g)[:]
                boxes.append((both[:, 0, :], both[:, 1, :], both))
            else:
                even = psum.tile([P, OUT_DIM], F32, tag="turn", bufs=TURN_BANKS, name="box_even")
                odd = psum.tile([P, OUT_DIM], F32, tag="product", bufs=Y_BANKS, name="box_odd")
                boxes.append((even[:], odd[:], None))
            for par in range(2):
                for dr in range(3):
                    nc.tensor.matmul(
                        out=boxes[g][par],
                        lhsT=col_sums[b][:, 1 - par, top + dr : top + dr + GROUP_ROWS, :].rearrange("f r m -> f (r m)"),
                        rhs=ident[:],
                        is_transpose=not (g in CLOCK_GROUPS and par == dr == 0),
                        start=(dr == 0),
                        stop=(dr == 2),
                    )

        def store(g):
            even, odd, both = boxes[g]
            d = d_out[:, group_kind(g), :]

            def scaled_on_scalar(par, box):
                nc.scalar.activation(out=out_sb[:, g, par, :], in_=box, func=ACT.Copy, scale=d[:, par : par + 1])

            if g == GROUPS - 1:
                scaled_on_scalar(0, even)
                nc.vector.tensor_scalar_mul(out=out_sb[:, g, 1, :], in0=odd, scalar1=d[:, 1:2])
            elif g in (0, 1, 2, 3):
                scaled_on_scalar(0, even)
                scaled_on_scalar(1, odd)
            else:
                nc.vector.tensor_mul(
                    out=out_sb[:, g, :, :], in0=both, in1=d.unsqueeze(2).to_broadcast([P, 2, OUT_DIM])
                )
            nc.sync.dma_start(out=out_groups[:, g, :], in_=out_sb[:, g, :, :].rearrange("p two f -> p (two f)"))

        relu_units = [(0, 0, 5), (0, 5, 9), (0, 9, 16), (0, 16, 24), (0, 24, 32), (1, 0, 8), (1, 8, 16), (1, 16, 24), (1, 24, 32)]
        sum_units = [(0, 0, 5), (0, 5, 9), (0, 9, 17), (0, 17, 25), (0, 25, 32), (1, 0, 9), (1, 9, 17), (1, 17, 25), (1, 25, 32)]
        AHEAD = 4
        BEHIND = 3
        affine_even(0, 16, 32)
        multiply_again_behind_vector(0)
        affine_even(1, 0, 16)
        multiply_again_behind_vector(1)
        for unit in relu_units[:AHEAD]:
            relu(*unit)
        sum_pairs(*sum_units[0])
        sum_pairs(*sum_units[1])
        multiply_again_behind_vector(2)
        for i in range(len(sum_units)):
            if i + AHEAD < len(relu_units):
                relu(*relu_units[i + AHEAD])
            if 1 < i < len(sum_units) - 1:
                sum_pairs(*sum_units[i + 1])
            sum_columns(*sum_units[i])
            if i == 1:
                sum_pairs(*sum_units[2])
            g = i - 1
            if g >= 0:
                sum_rows(g)
            if g >= BEHIND:
                store(g - BEHIND)
        for g in range(GROUPS - BEHIND, GROUPS):
            store(g)
